import numpy as np
import ml_dtypes


def mxq(x, axis, fmt="e4m3"):
    dtype, down = {"e4m3": (ml_dtypes.float8_e4m3fn, 7), "e5m2": (ml_dtypes.float8_e5m2, 14)}[fmt]
    v = np.moveaxis(np.asarray(x, np.float32).astype(ml_dtypes.bfloat16).astype(np.float64), axis, -1)
    blocks = v.reshape(v.shape[:-1] + (-1, 32))
    amax = np.abs(blocks).max(-1, keepdims=True)
    byte = np.maximum(np.where(amax > 0, np.frexp(amax)[1] - 1 + 127, 0) - down, 1)
    scale = np.exp2(byte - 127.0)
    codes = (blocks / scale).astype(np.float32).astype(dtype).astype(np.float64)
    return np.moveaxis((codes * scale).reshape(v.shape), -1, axis)


WIDE = False


def mx_kscale(k):
    if not WIDE:
        return np.ones(k)
    levels = np.array([10, -10, 5, -5, 0])
    if k % 512:
        return np.exp2(np.random.permutation(np.resize(levels, k // 32))).repeat(32)
    a = np.empty((k // 512, 16))
    for p in range(k // 512):
        a[p, :8] = np.random.permutation(np.resize(levels, 8))
        for g in range(8):
            far = levels[np.abs(levels - a[p, g]) >= 10]
            a[p, g + 8] = far[np.random.randint(len(far))]
    return np.exp2(a.ravel()).repeat(32)


BF16 = ml_dtypes.bfloat16


def bf(x):
    return np.asarray(x, np.float32).astype(BF16)


def f64(x):
    return np.asarray(x).astype(np.float64)


B, HEAD, NUM_EXPERTS, HEAD_DIM = 4096, 1, 3, 512
EPS = 1e-5
VAR0 = 3e-4


def setup_inputs():
    s = mx_kscale(HEAD_DIM)
    p = (HEAD, NUM_EXPERTS, HEAD_DIM)

    def draw_x():
        return bf((np.random.standard_normal((B, HEAD, HEAD_DIM)) * s).reshape(B, HEAD * HEAD_DIM))

    return {"x1": draw_x(), "x2": draw_x(), "x3": draw_x(),
            "W": bf(np.random.standard_normal((HEAD, NUM_EXPERTS, HEAD_DIM, HEAD_DIM)) / np.sqrt(HEAD_DIM) / s),
            "b": bf(np.random.standard_normal(p) * 0.3),
            "gamma": bf(np.sqrt(VAR0) * (1.0 + 0.1 * np.random.standard_normal(p))),
            "beta": bf(np.random.standard_normal(p) * 0.3),
            "running_mean": bf(np.random.standard_normal(p) * 0.3),
            "running_var": bf(VAR0 * np.random.uniform(0.5, 1.5, p))}


def reference(x1, x2, x3, W, b, gamma, beta, running_mean, running_var):
    n = x1.shape[0]
    xs = np.stack([f64(x1).reshape(n, HEAD, HEAD_DIM),
                   f64(x2).reshape(n, HEAD, HEAD_DIM),
                   f64(x3).reshape(n, HEAD, HEAD_DIM)], axis=2)
    xq = mxq(xs, 3, "e4m3")
    wq = mxq(f64(W), 3, "e4m3")
    y = (xq.transpose(1, 2, 0, 3) @ wq.transpose(0, 1, 3, 2)).transpose(2, 0, 1, 3) + f64(b)
    y = y * (1.0 / (1.0 + np.exp(-1.702 * y)))
    y = (y - f64(running_mean)) * (1.0 / np.sqrt(f64(running_var) + EPS)) * f64(gamma) + f64(beta)
    return np.transpose(y, (0, 2, 1, 3)).reshape(n, NUM_EXPERTS * HEAD * HEAD_DIM)

@@ -1,0 +1,232 @@
+from contextlib import ExitStack
+
+import concourse.mybir as mybir
+from concourse.masks import make_identity
+
+F32 = mybir.dt.float32
+BF16 = mybir.dt.bfloat16
+U32 = mybir.dt.uint32
+U8 = mybir.dt.uint8
+FP8X4 = mybir.dt.float8_e4m3fn_x4
+ACT = mybir.ActivationFunctionType
+ALU = mybir.AluOpType
+
+P = 128
+TOKENS = 4096
+D = 512
+E = 3
+EPS = 1e-5
+JT = TOKENS // P
+TB = 8
+NR = TB * E
+FLOPS = 2 * TOKENS * D * D * E
+
+X_BUFS = 20
+PREFETCH = 16
+
+
+def tile_mom_t_kernel(tc, x1, x2, x3, W, b, gamma, beta, running_mean, running_var, out):
+    nc = tc.nc
+    xs = [x.rearrange("(p j) k -> p (j k)", j=JT) for x in (x1, x2, x3)]
+    w_rows = W.rearrange("o e f k -> (o e f) k")
+    out_v = out.rearrange("(p j) c -> p j c", j=JT)
+
+    with ExitStack() as ctx:
+        const = ctx.enter_context(tc.tile_pool(name="const", bufs=1))
+        xin_pool = ctx.enter_context(tc.tile_pool(name="xin", bufs=X_BUFS))
+        grp_pool = ctx.enter_context(tc.tile_pool(name="grp", bufs=3))
+        q_pool = ctx.enter_context(tc.tile_pool(name="q", bufs=3))
+        z_pool = ctx.enter_context(tc.tile_pool(name="z", bufs=3))
+        st_pool = ctx.enter_context(tc.tile_pool(name="st", bufs=3))
+        psum = ctx.enter_context(tc.psum_pool(name="psum", bufs=8))
+        ctx.enter_context(tc.manual_schedule())
+
+        ident = const.tile([P, P], F32, name="ident")
+        make_identity(nc, ident[:])
+
+        prow = const.tile([P, P], BF16, name="prow")
+        nc.vector.memset(prow[:], 0.0)
+        for i, v in enumerate((b, gamma, beta, running_mean, running_var)):
+            nc.scalar.dma_start(out=prow[16 * i : 16 * i + 12, :], in_=v.rearrange("o e (q c) -> (o e q) c", c=P))
+
+        xin = {}
+        win = {}
+
+        def load_w(e):
+            t = xin_pool.tile([P, 4 * D], BF16, name="win%d" % e, tag="xin")
+            cuts = (0, 1, 2, 4) if e == 0 else (0, 4)
+            for lo, hi in zip(cuts[:-1], cuts[1:]):
+                nc.sync.dma_start(
+                    out=t[:].rearrange("p (q k) -> p q k", q=4)[:, lo:hi, :],
+                    in_=w_rows[e * D + lo * P : e * D + hi * P, :].rearrange("(q p) k -> p q k", p=P),
+                )
+            win[e] = t
+
+        def load_x(r):
+            tb, e = divmod(r, E)
+            t = xin_pool.tile([P, 4 * D], BF16, name="xin%d" % r, tag="xin")
+            cuts = (0, 2, 4) if r == 0 else (0, 4)
+            for lo, hi in zip(cuts[:-1], cuts[1:]):
+                nc.sync.dma_start(out=t[:, lo * D : hi * D], in_=xs[e][:, (tb * 4 + lo) * D : (tb * 4 + hi) * D])
+            xin[r] = t
+
+        for e in range(E):
+            load_w(e)
+            load_x(e)
+        for r in range(E, PREFETCH):
+            load_x(r)
+
+        w_codes = [const.tile([P, D], U32, name="wc%d" % e, align_bytes=64) for e in range(E)]
+        w_scales = [const.tile([P, D], U8, name="ws%d" % e, align_bytes=64) for e in range(E)]
+        grouped = {}
+        codes = {}
+        scales = {}
+        zt = {}
+        stage = {}
+        par = {}
+
+        def transposes_in(src, key, on_scalar):
+            sf = src[:].bitcast(F32)
+            g = grp_pool.tile([P, 4 * D], BF16, name="g_%s" % key, tag="g", align_bytes=64)
+            gf = g[:].bitcast(F32)
+            banks = []
+            for h in range(2):
+                bank = psum.tile([P, D], F32, name="a_%s_%d" % (key, h), tag="bank")
+                for jj in (2 * h, 2 * h + 1):
+                    for u in range(2):
+                        nc.tensor.transpose(
+                            bank[:, u * 256 + (jj % 2) * P : u * 256 + (jj % 2) * P + P],
+                            sf[:, jj * 256 + u : (jj + 1) * 256 : 2],
+                            ident[:],
+                        )
+                banks.append(bank)
+            for h in range(2):
+                dst = gf[:, h * D : (h + 1) * D].rearrange("p (c u) -> p c u", u=2)
+                srcv = banks[h][:].rearrange("p (u c) -> p c u", u=2)
+                if h == 1 and on_scalar:
+                    nc.scalar.copy(out=dst, in_=srcv)
+                else:
+                    nc.vector.tensor_copy(out=dst, in_=srcv)
+            return g
+
+        def params_transpose():
+            pf = const.tile([P, P], F32, name="pf")
+            nc.vector.tensor_copy(out=pf[:], in_=prow[:])
+            bank = psum.tile([P, D], F32, name="pbank", tag="bank")
+            nc.tensor.transpose(bank[:, 0:P], pf[:], ident[:])
+            par["bank"] = bank
+
+        def params_sqrt():
+            pt = const.tile([P, P], F32, name="pt")
+            nc.vector.tensor_copy(out=pt[:], in_=par["bank"][:, 0:P])
+            sd = const.tile([P, 12], F32, name="sd")
+            nc.vector.tensor_scalar_add(out=sd[:], in0=pt[:, 64:76], scalar1=EPS)
+            nc.scalar.activation(out=sd[:], in_=sd[:], func=ACT.Sqrt)
+            par["b"] = pt
+            par["sd"] = sd
+
+        def params_affine():
+            pt = par["b"]
+            s_t = const.tile([P, 12], F32, name="s_t")
+            nc.vector.reciprocal(out=s_t[:], in_=par["sd"][:])
+            nc.vector.tensor_mul(out=s_t[:], in0=s_t[:], in1=pt[:, 16:28])
+            t_t = const.tile([P, 12], F32, name="t_t")
+            nc.vector.tensor_mul(out=t_t[:], in0=pt[:, 48:60], in1=s_t[:])
+            nc.vector.tensor_sub(out=t_t[:], in0=pt[:, 32:44], in1=t_t[:])
+            par["s"] = s_t
+            par["t"] = t_t
+
+        def store(tb, lo, hi, c0, c1):
+            nc.sync.dma_start(
+                out=out_v[:, tb * 4 + lo : tb * 4 + hi, c0:c1],
+                in_=stage[tb][:].rearrange("p (j c) -> p j c", j=4)[:, lo:hi, c0:c1],
+            )
+
+        for s in range(-2, NR + 1):
+            if 0 <= s < NR:
+                e = s % E
+                z = z_pool.tile([P, 4, D], F32, name="z%d" % s, tag="z")
+                zt[s] = z
+                accs = []
+                for fb in range(4):
+                    acc = psum.tile([P, D], F32, name="acc%d_%d" % (s, fb), tag="bank")
+                    nc.tensor.matmul_mx(
+                        out=acc[:],
+                        lhsT=w_codes[e][:, fb * P : (fb + 1) * P].bitcast(FP8X4),
+                        lhsT_scale=w_scales[e][:, fb * P : (fb + 1) * P],
+                        rhs=codes[s][:].bitcast(FP8X4),
+                        rhs_scale=scales[s][:],
+                        start=True,
+                        stop=True,
+                    )
+                    accs.append(acc)
+                for fb in range(4):
+                    col = e * 4 + fb
+                    nc.scalar.activation(
+                        out=z[:, fb, :], in_=accs[fb][:], func=ACT.Gelu_apprx_sigmoid,
+                        bias=par["b"][:, col : col + 1], scale=1.0,
+                    )
+                for fb in range(4):
+                    col = e * 4 + fb
+                    eng = nc.vector if (s == NR - 1 and fb >= 2) else nc.gpsimd
+                    eng.tensor_scalar(
+                        out=z[:, fb, :], in0=z[:, fb, :],
+                        scalar1=par["s"][:, col : col + 1], scalar2=par["t"][:, col : col + 1],
+                        op0=ALU.mult, op1=ALU.add,
+                    )
+            q = s + 1
+            if 0 <= q < E:
+                nc.vector.quantize_mx(out=w_codes[q][:].bitcast(FP8X4), scales=w_scales[q][:], in_=grouped["w%d" % q][:])
+            if 0 <= q < NR:
+                c_t = q_pool.tile([P, D], U32, name="c%d" % q, tag="c", align_bytes=64)
+                s_t2 = q_pool.tile([P, D], U8, name="s%d" % q, tag="s", align_bytes=64)
+                nc.vector.quantize_mx(out=c_t[:].bitcast(FP8X4), scales=s_t2[:], in_=grouped[q][:])
+                codes[q] = c_t
+                scales[q] = s_t2
+            if s == -1:
+                params_sqrt()
+            a = s + 2
+            if 0 <= a < E:
+                grouped["w%d" % a] = transposes_in(win[a], "w%d" % a, True)
+            if 0 <= a < NR:
+                grouped[a] = transposes_in(xin[a], "x%d" % a, a < 3)
+            if s == -2:
+                params_transpose()
+            if s == -1:
+                params_affine()
+            o = s - 1
+            if 0 <= o < NR:
+                tb, e = divmod(o, E)
+                if e == 0:
+                    stage[tb] = st_pool.tile([P, 4 * E * D], F32, name="st%d" % tb, tag="st")
+                banks = []
+                for jj in range(4):
+                    bank = psum.tile([P, D], F32, name="o%d_%d" % (o, jj), tag="bank")
+                    for fb in range(4):
+                        nc.tensor.transpose(bank[:, fb * P : (fb + 1) * P], zt[o][:, fb, jj * P : (jj + 1) * P], ident[:])
+                    banks.append(bank)
+                if o == NR - 1:
+                    on_scalar = (0, 2)
+                elif o % 2 == 1:
+                    on_scalar = (0, 1)
+                else:
+                    on_scalar = (0,)
+                for jj in range(4):
+                    dst = stage[tb][:, jj * E * D + e * D : jj * E * D + (e + 1) * D]
+                    if jj in on_scalar:
+                        nc.scalar.copy(out=dst, in_=banks[jj][:])
+                    else:
+                        nc.vector.tensor_copy(out=dst, in_=banks[jj][:])
+            ld = s + PREFETCH
+            if PREFETCH <= ld < NR:
+                load_x(ld)
+            if 0 <= o < NR:
+                tb, e = divmod(o, E)
+                if tb < TB - 1:
+                    if e == E - 1:
+                        store(tb, 0, 4, 0, E * D)
+                elif e < E - 1:
+                    store(tb, 0, 4, e * D, (e + 1) * D)
+                else:
+                    for jj in range(4):
+                        store(tb, jj, jj + 1, e * D, (e + 1) * D)

@@ -41,8 +41,14 @@ def tile_mom_t_kernel(tc, x1, x2, x3, W, b, gamma, beta, running_mean, running_v
         psum = ctx.enter_context(tc.psum_pool(name="psum", bufs=8))
         ctx.enter_context(tc.manual_schedule())
 
+        warm = const.tile([P, 1], F32, name="warm")
+        nc.vector.memset(warm[:], 0.0)
+        nc.scalar.activation(out=warm[:], in_=warm[:], func=ACT.Gelu_apprx_sigmoid)
+
         ident = const.tile([P, P], F32, name="ident")
         make_identity(nc, ident[:])
+        mhalf = const.tile([P, 12], F32, name="mhalf")
+        nc.gpsimd.memset(mhalf[:], -0.5)
 
         prow = const.tile([P, P], BF16, name="prow")
         nc.vector.memset(prow[:], 0.0)
@@ -85,7 +91,7 @@ def tile_mom_t_kernel(tc, x1, x2, x3, W, b, gamma, beta, running_mean, running_v
         stage = {}
         par = {}
 
-        def transposes_in(src, key, on_scalar):
+        def transposes_in(src, key, engines):
             sf = src[:].bitcast(F32)
             g = grp_pool.tile([P, 4 * D], BF16, name="g_%s" % key, tag="g", align_bytes=64)
             gf = g[:].bitcast(F32)
@@ -101,40 +107,113 @@ def tile_mom_t_kernel(tc, x1, x2, x3, W, b, gamma, beta, running_mean, running_v
                         )
                 banks.append(bank)
             for h in range(2):
-                dst = gf[:, h * D : (h + 1) * D].rearrange("p (c u) -> p c u", u=2)
-                srcv = banks[h][:].rearrange("p (u c) -> p c u", u=2)
-                if h == 1 and on_scalar:
-                    nc.scalar.copy(out=dst, in_=srcv)
-                else:
-                    nc.vector.tensor_copy(out=dst, in_=srcv)
-            return g
+                copy_bank(engines[h], gf[:, h * D : (h + 1) * D].rearrange("p (c u) -> p c u", u=2),
+                          banks[h][:].rearrange("p (u c) -> p c u", u=2))
+            grouped[key] = g
+
+        def copy_bank(engine, dst, src):
+            if engine == "S":
+                nc.scalar.copy(out=dst, in_=src)
+            else:
+                nc.vector.tensor_copy(out=dst, in_=src)
+
+        def quantise_w(e):
+            nc.vector.quantize_mx(out=w_codes[e][:].bitcast(FP8X4), scales=w_scales[e][:], in_=grouped["w%d" % e][:])
+
+        def quantise_x(q):
+            c_t = q_pool.tile([P, D], U32, name="c%d" % q, tag="c", align_bytes=64)
+            s_t2 = q_pool.tile([P, D], U8, name="s%d" % q, tag="s", align_bytes=64)
+            nc.vector.quantize_mx(out=c_t[:].bitcast(FP8X4), scales=s_t2[:], in_=grouped["x%d" % q][:])
+            codes[q] = c_t
+            scales[q] = s_t2
 
         def params_transpose():
-            pf = const.tile([P, P], F32, name="pf")
-            nc.vector.tensor_copy(out=pf[:], in_=prow[:])
             bank = psum.tile([P, D], F32, name="pbank", tag="bank")
-            nc.tensor.transpose(bank[:, 0:P], pf[:], ident[:])
+            nc.tensor.transpose(bank[:, 0:P], par["pf"][:], ident[:])
             par["bank"] = bank
 
-        def params_sqrt():
-            pt = const.tile([P, P], F32, name="pt")
-            nc.vector.tensor_copy(out=pt[:], in_=par["bank"][:, 0:P])
-            sd = const.tile([P, 12], F32, name="sd")
-            nc.vector.tensor_scalar_add(out=sd[:], in0=pt[:, 64:76], scalar1=EPS)
-            nc.scalar.activation(out=sd[:], in_=sd[:], func=ACT.Sqrt)
-            par["b"] = pt
-            par["sd"] = sd
+        def params_cast():
+            pf = const.tile([P, P], F32, name="pf")
+            nc.vector.tensor_copy(out=pf[:], in_=prow[:])
+            par["pf"] = pf
 
         def params_affine():
-            pt = par["b"]
+            pt = const.tile([P, P], F32, name="pt")
+            nc.vector.tensor_copy(out=pt[:], in_=par["bank"][:, 0:P])
             s_t = const.tile([P, 12], F32, name="s_t")
-            nc.vector.reciprocal(out=s_t[:], in_=par["sd"][:])
-            nc.vector.tensor_mul(out=s_t[:], in0=s_t[:], in1=pt[:, 16:28])
+            nc.gpsimd.tensor_scalar_add(out=s_t[:], in0=pt[:, 64:76], scalar1=EPS)
+            nc.gpsimd.tensor_tensor(out=s_t[:], in0=s_t[:], in1=mhalf[:], op=ALU.pow)
+            nc.gpsimd.tensor_mul(out=s_t[:], in0=s_t[:], in1=pt[:, 16:28])
             t_t = const.tile([P, 12], F32, name="t_t")
-            nc.vector.tensor_mul(out=t_t[:], in0=pt[:, 48:60], in1=s_t[:])
-            nc.vector.tensor_sub(out=t_t[:], in0=pt[:, 32:44], in1=t_t[:])
+            nc.gpsimd.tensor_mul(out=t_t[:], in0=pt[:, 48:60], in1=s_t[:])
+            nc.gpsimd.tensor_sub(out=t_t[:], in0=pt[:, 32:44], in1=t_t[:])
+            par["b"] = pt
             par["s"] = s_t
             par["t"] = t_t
+
+        accs = {}
+
+        def products(s):
+            e = s % E
+            accs[s] = []
+            for fb in range(4):
+                acc = psum.tile([P, D], F32, name="acc%d_%d" % (s, fb), tag="bank")
+                nc.tensor.matmul_mx(
+                    out=acc[:],
+                    lhsT=w_codes[e][:, fb * P : (fb + 1) * P].bitcast(FP8X4),
+                    lhsT_scale=w_scales[e][:, fb * P : (fb + 1) * P],
+                    rhs=codes[s][:].bitcast(FP8X4),
+                    rhs_scale=scales[s][:],
+                    start=True,
+                    stop=True,
+                )
+                accs[s].append(acc)
+
+        def gelu(s, fb, t0, t1):
+            col = s % E * 4 + fb
+            nc.scalar.activation(
+                out=zt[s][:, fb, t0:t1], in_=accs[s][fb][:, t0:t1], func=ACT.Gelu_apprx_sigmoid,
+                bias=par["b"][:, col : col + 1], scale=1.0,
+            )
+
+        def affine(engine, s, fb, t0, t1):
+            col = s % E * 4 + fb
+            engine.tensor_scalar(
+                out=zt[s][:, fb, t0:t1], in0=zt[s][:, fb, t0:t1],
+                scalar1=par["s"][:, col : col + 1], scalar2=par["t"][:, col : col + 1],
+                op0=ALU.mult, op1=ALU.add,
+            )
+
+        def activate(s):
+            zt[s] = z_pool.tile([P, 4, D], F32, name="z%d" % s, tag="z")
+            for fb in range(4):
+                gelu(s, fb, 0, D)
+            for fb in range(4):
+                affine(nc.gpsimd, s, fb, 0, D)
+
+        def out_bank(o, jj):
+            bank = psum.tile([P, D], F32, name="o%d_%d" % (o, jj), tag="bank")
+            return bank
+
+        def back_transpose(o, bank, jj, fb):
+            nc.tensor.transpose(bank[:, fb * P : (fb + 1) * P], zt[o][:, fb, jj * P : (jj + 1) * P], ident[:])
+
+        def out_copy(o, bank, jj, engine):
+            tb, e = divmod(o, E)
+            copy_bank(engine, stage[tb][:, jj * E * D + e * D : jj * E * D + (e + 1) * D], bank[:])
+
+        def transposes_out(o, on_scalar):
+            tb, e = divmod(o, E)
+            if e == 0:
+                stage[tb] = st_pool.tile([P, 4 * E * D], F32, name="st%d" % tb, tag="st")
+            banks = []
+            for jj in range(4):
+                bank = out_bank(o, jj)
+                for fb in range(4):
+                    back_transpose(o, bank, jj, fb)
+                banks.append(bank)
+            for jj in range(4):
+                out_copy(o, banks[jj], jj, "S" if jj in on_scalar else "V")
 
         def store(tb, lo, hi, c0, c1):
             nc.sync.dma_start(
@@ -142,91 +221,64 @@ def tile_mom_t_kernel(tc, x1, x2, x3, W, b, gamma, beta, running_mean, running_v
                 in_=stage[tb][:].rearrange("p (j c) -> p j c", j=4)[:, lo:hi, c0:c1],
             )
 
-        for s in range(-2, NR + 1):
-            if 0 <= s < NR:
-                e = s % E
-                z = z_pool.tile([P, 4, D], F32, name="z%d" % s, tag="z")
-                zt[s] = z
-                accs = []
-                for fb in range(4):
-                    acc = psum.tile([P, D], F32, name="acc%d_%d" % (s, fb), tag="bank")
-                    nc.tensor.matmul_mx(
-                        out=acc[:],
-                        lhsT=w_codes[e][:, fb * P : (fb + 1) * P].bitcast(FP8X4),
-                        lhsT_scale=w_scales[e][:, fb * P : (fb + 1) * P],
-                        rhs=codes[s][:].bitcast(FP8X4),
-                        rhs_scale=scales[s][:],
-                        start=True,
-                        stop=True,
-                    )
-                    accs.append(acc)
-                for fb in range(4):
-                    col = e * 4 + fb
-                    nc.scalar.activation(
-                        out=z[:, fb, :], in_=accs[fb][:], func=ACT.Gelu_apprx_sigmoid,
-                        bias=par["b"][:, col : col + 1], scale=1.0,
-                    )
-                for fb in range(4):
-                    col = e * 4 + fb
-                    eng = nc.vector if (s == NR - 1 and fb >= 2) else nc.gpsimd
-                    eng.tensor_scalar(
-                        out=z[:, fb, :], in0=z[:, fb, :],
-                        scalar1=par["s"][:, col : col + 1], scalar2=par["t"][:, col : col + 1],
-                        op0=ALU.mult, op1=ALU.add,
-                    )
-            q = s + 1
-            if 0 <= q < E:
-                nc.vector.quantize_mx(out=w_codes[q][:].bitcast(FP8X4), scales=w_scales[q][:], in_=grouped["w%d" % q][:])
-            if 0 <= q < NR:
-                c_t = q_pool.tile([P, D], U32, name="c%d" % q, tag="c", align_bytes=64)
-                s_t2 = q_pool.tile([P, D], U8, name="s%d" % q, tag="s", align_bytes=64)
-                nc.vector.quantize_mx(out=c_t[:].bitcast(FP8X4), scales=s_t2[:], in_=grouped[q][:])
-                codes[q] = c_t
-                scales[q] = s_t2
-            if s == -1:
-                params_sqrt()
-            a = s + 2
-            if 0 <= a < E:
-                grouped["w%d" % a] = transposes_in(win[a], "w%d" % a, True)
-            if 0 <= a < NR:
-                grouped[a] = transposes_in(xin[a], "x%d" % a, a < 3)
-            if s == -2:
-                params_transpose()
-            if s == -1:
-                params_affine()
+        def store_round(o):
+            tb, e = divmod(o, E)
+            if tb >= TB - 2:
+                store(tb, 0, 4, e * D, (e + 1) * D)
+            elif e == E - 1:
+                store(tb, 0, 4, 0, E * D)
+
+        transposes_in(win[0], "w0", "VS")
+        transposes_in(xin[0], "x0", "VS")
+        transposes_in(win[1], "w1", "SS")
+        params_cast()
+        quantise_w(0)
+        quantise_x(0)
+        params_transpose()
+        params_affine()
+        products(0)
+        activate(0)
+        transposes_in(xin[1], "x1", "VV")
+        quantise_w(1)
+        quantise_x(1)
+        transposes_in(win[2], "w2", "SS")
+        transposes_in(xin[2], "x2", "VV")
+
+        load_x(PREFETCH)
+
+        for s in range(1, NR - 1):
+            products(s)
+            activate(s)
+            if s + 1 == 2:
+                quantise_w(2)
+            quantise_x(s + 1)
+            if s + 2 < NR:
+                transposes_in(xin[s + 2], "x%d" % (s + 2), "VV")
             o = s - 1
-            if 0 <= o < NR:
-                tb, e = divmod(o, E)
-                if e == 0:
-                    stage[tb] = st_pool.tile([P, 4 * E * D], F32, name="st%d" % tb, tag="st")
-                banks = []
-                for jj in range(4):
-                    bank = psum.tile([P, D], F32, name="o%d_%d" % (o, jj), tag="bank")
-                    for fb in range(4):
-                        nc.tensor.transpose(bank[:, fb * P : (fb + 1) * P], zt[o][:, fb, jj * P : (jj + 1) * P], ident[:])
-                    banks.append(bank)
-                if o == NR - 1:
-                    on_scalar = (0, 2)
-                elif o % 2 == 1:
-                    on_scalar = (0, 1)
-                else:
-                    on_scalar = (0,)
-                for jj in range(4):
-                    dst = stage[tb][:, jj * E * D + e * D : jj * E * D + (e + 1) * D]
-                    if jj in on_scalar:
-                        nc.scalar.copy(out=dst, in_=banks[jj][:])
-                    else:
-                        nc.vector.tensor_copy(out=dst, in_=banks[jj][:])
-            ld = s + PREFETCH
-            if PREFETCH <= ld < NR:
-                load_x(ld)
-            if 0 <= o < NR:
-                tb, e = divmod(o, E)
-                if tb < TB - 1:
-                    if e == E - 1:
-                        store(tb, 0, 4, 0, E * D)
-                elif e < E - 1:
-                    store(tb, 0, 4, e * D, (e + 1) * D)
-                else:
-                    for jj in range(4):
-                        store(tb, jj, jj + 1, e * D, (e + 1) * D)
+            transposes_out(o, (0, 1) if o % 2 == 1 else (0,))
+            if s + PREFETCH < NR:
+                load_x(s + PREFETCH)
+            store_round(o)
+
+        s = NR - 1
+        products(s)
+        zt[s] = z_pool.tile([P, 4, D], F32, name="z%d" % s, tag="z")
+        H = D // 2
+        for half in range(2):
+            for fb in range(4):
+                gelu(s, fb, half * H, half * H + H)
+        for fb in range(4):
+            affine(nc.gpsimd, s, fb, 0, H)
+        transposes_out(s - 1, ())
+        store_round(s - 1)
+        for fb in range(4):
+            affine(nc.vector, s, fb, H, D)
+        for half in range(2):
+            banks = [out_bank(s, 2 * half + i) for i in range(2)]
+            for fb in range(4):
+                for i in range(2):
+                    back_transpose(s, banks[i], 2 * half + i, fb)
+            for i in range(2):
+                jj = 2 * half + i
+                out_copy(s, banks[i], jj, "VS"[i])
+                store(TB - 1, jj, jj + 1, 2 * D, 3 * D)

@@ -23,6 +23,7 @@ FLOPS = 2 * TOKENS * D * D * E
 
 X_BUFS = 20
 PREFETCH = 16
+ON_VECTOR = (3,)
 
 
 def tile_mom_t_kernel(tc, x1, x2, x3, W, b, gamma, beta, running_mean, running_var, out):
@@ -189,7 +190,12 @@ def tile_mom_t_kernel(tc, x1, x2, x3, W, b, gamma, beta, running_mean, running_v
             for fb in range(4):
                 gelu(s, fb, 0, D)
             for fb in range(4):
-                affine(nc.gpsimd, s, fb, 0, D)
+                if fb not in ON_VECTOR:
+                    affine(nc.gpsimd, s, fb, 0, D)
+
+        def affine_on_vector(s):
+            for fb in ON_VECTOR:
+                affine(nc.vector, s, fb, 0, D)
 
         def out_bank(o, jj):
             bank = psum.tile([P, D], F32, name="o%d_%d" % (o, jj), tag="bank")
@@ -241,6 +247,7 @@ def tile_mom_t_kernel(tc, x1, x2, x3, W, b, gamma, beta, running_mean, running_v
         transposes_in(xin[1], "x1", "VV")
         quantise_w(1)
         quantise_x(1)
+        affine_on_vector(0)
         transposes_in(win[2], "w2", "SS")
         transposes_in(xin[2], "x2", "VV")
 
@@ -255,7 +262,8 @@ def tile_mom_t_kernel(tc, x1, x2, x3, W, b, gamma, beta, running_mean, running_v
             if s + 2 < NR:
                 transposes_in(xin[s + 2], "x%d" % (s + 2), "VV")
             o = s - 1
-            transposes_out(o, (0, 1) if o % 2 == 1 else (0,))
+            transposes_out(o, (0, 1))
+            affine_on_vector(s)
             if s + PREFETCH < NR:
                 load_x(s + PREFETCH)
             store_round(o)

@@ -135,12 +135,12 @@ def tile_mom_t_kernel(tc, x1, x2, x3, W, b, gamma, beta, running_mean, running_v
 
         def params_cast():
             pf = const.tile([P, P], F32, name="pf")
-            nc.vector.tensor_copy(out=pf[:], in_=prow[:])
+            nc.gpsimd.tensor_copy(out=pf[:], in_=prow[:])
             par["pf"] = pf
 
         def params_affine():
             pt = const.tile([P, P], F32, name="pt")
-            nc.vector.tensor_copy(out=pt[:], in_=par["bank"][:, 0:P])
+            nc.scalar.copy(out=pt[:], in_=par["bank"][:, 0:P])
             s_t = const.tile([P, 12], F32, name="s_t")
             nc.gpsimd.tensor_scalar_add(out=s_t[:], in0=pt[:, 64:76], scalar1=EPS)
             nc.gpsimd.tensor_tensor(out=s_t[:], in0=s_t[:], in1=mhalf[:], op=ALU.pow)
@@ -234,12 +234,12 @@ def tile_mom_t_kernel(tc, x1, x2, x3, W, b, gamma, beta, running_mean, running_v
             elif e == E - 1:
                 store(tb, 0, 4, 0, E * D)
 
+        params_cast()
         transposes_in(win[0], "w0", "VS")
         transposes_in(xin[0], "x0", "VS")
-        transposes_in(win[1], "w1", "SS")
-        params_cast()
         quantise_w(0)
         quantise_x(0)
+        transposes_in(win[1], "w1", "SS")
         params_transpose()
         params_affine()
         products(0)
@@ -262,7 +262,7 @@ def tile_mom_t_kernel(tc, x1, x2, x3, W, b, gamma, beta, running_mean, running_v
             if s + 2 < NR:
                 transposes_in(xin[s + 2], "x%d" % (s + 2), "VV")
             o = s - 1
-            transposes_out(o, (0, 1))
+            transposes_out(o, (0, 1) if o % 2 == 1 else (0,))
             affine_on_vector(s)
             if s + PREFETCH < NR:
                 load_x(s + PREFETCH)

@@ -262,7 +262,7 @@ def tile_mom_t_kernel(tc, x1, x2, x3, W, b, gamma, beta, running_mean, running_v
             if s + 2 < NR:
                 transposes_in(xin[s + 2], "x%d" % (s + 2), "VV")
             o = s - 1
-            transposes_out(o, (0, 1) if o % 2 == 1 else (0,))
+            transposes_out(o, (0, 1))
             affine_on_vector(s)
             if s + PREFETCH < NR:
                 load_x(s + PREFETCH)

@@ -46,6 +46,12 @@ def tile_mom_t_kernel(tc, x1, x2, x3, W, b, gamma, beta, running_mean, running_v
         nc.vector.memset(warm[:], 0.0)
         nc.scalar.activation(out=warm[:], in_=warm[:], func=ACT.Gelu_apprx_sigmoid)
 
+        zeros = const.tile([P, D], BF16, name="zeros")
+        nc.gpsimd.memset(zeros[:], 0.0)
+        idle = psum.tile([P, D], F32, name="idle", tag="bank")
+        for i in range(2):
+            nc.tensor.matmul(idle[:], lhsT=zeros[:, 0:P], rhs=zeros[:], start=True, stop=True)
+
         ident = const.tile([P, P], F32, name="ident")
         make_identity(nc, ident[:])
         mhalf = const.tile([P, 12], F32, name="mhalf")
@@ -138,19 +144,22 @@ def tile_mom_t_kernel(tc, x1, x2, x3, W, b, gamma, beta, running_mean, running_v
             nc.gpsimd.tensor_copy(out=pf[:], in_=prow[:])
             par["pf"] = pf
 
-        def params_affine():
+        def params_columns():
             pt = const.tile([P, P], F32, name="pt")
             nc.scalar.copy(out=pt[:], in_=par["bank"][:, 0:P])
-            s_t = const.tile([P, 12], F32, name="s_t")
-            nc.gpsimd.tensor_scalar_add(out=s_t[:], in0=pt[:, 64:76], scalar1=EPS)
-            nc.gpsimd.tensor_tensor(out=s_t[:], in0=s_t[:], in1=mhalf[:], op=ALU.pow)
-            nc.gpsimd.tensor_mul(out=s_t[:], in0=s_t[:], in1=pt[:, 16:28])
-            t_t = const.tile([P, 12], F32, name="t_t")
-            nc.gpsimd.tensor_mul(out=t_t[:], in0=pt[:, 48:60], in1=s_t[:])
-            nc.gpsimd.tensor_sub(out=t_t[:], in0=pt[:, 32:44], in1=t_t[:])
             par["b"] = pt
-            par["s"] = s_t
-            par["t"] = t_t
+            par["s"] = const.tile([P, 12], F32, name="s_t")
+            par["t"] = const.tile([P, 12], F32, name="t_t")
+
+        def params_affine(c0, c1):
+            pt = par["b"]
+            s_t = par["s"][:, c0:c1]
+            t_t = par["t"][:, c0:c1]
+            nc.gpsimd.tensor_scalar_add(out=s_t, in0=pt[:, 64 + c0 : 64 + c1], scalar1=EPS)
+            nc.gpsimd.tensor_tensor(out=s_t, in0=s_t, in1=mhalf[:, c0:c1], op=ALU.pow)
+            nc.gpsimd.tensor_mul(out=s_t, in0=s_t, in1=pt[:, 16 + c0 : 16 + c1])
+            nc.gpsimd.tensor_mul(out=t_t, in0=pt[:, 48 + c0 : 48 + c1], in1=s_t)
+            nc.gpsimd.tensor_sub(out=t_t, in0=pt[:, 32 + c0 : 32 + c1], in1=t_t)
 
         accs = {}
 
@@ -240,18 +249,23 @@ def tile_mom_t_kernel(tc, x1, x2, x3, W, b, gamma, beta, running_mean, running_v
         quantise_w(0)
         quantise_x(0)
         transposes_in(win[1], "w1", "SS")
-        params_transpose()
-        params_affine()
-        products(0)
-        activate(0)
         transposes_in(xin[1], "x1", "VV")
         quantise_w(1)
+        params_transpose()
+        params_columns()
+        params_affine(0, 4)
+        params_affine(4, 12)
+        products(0)
+        zt[0] = z_pool.tile([P, 4, D], F32, name="z0", tag="z")
+        for fb in range(4):
+            gelu(0, fb, 0, D)
         quantise_x(1)
-        affine_on_vector(0)
-        transposes_in(win[2], "w2", "SS")
+        transposes_in(win[2], "w2", "SV")
         transposes_in(xin[2], "x2", "VV")
-
-        load_x(PREFETCH)
+        for fb in range(4):
+            affine(nc.vector, 0, fb, 0, D)
+        for r in range(PREFETCH, PREFETCH + 4):
+            load_x(r)
 
         for s in range(1, NR - 1):
             products(s)
@@ -264,8 +278,8 @@ def tile_mom_t_kernel(tc, x1, x2, x3, W, b, gamma, beta, running_mean, running_v
             o = s - 1
             transposes_out(o, (0, 1))
             affine_on_vector(s)
-            if s + PREFETCH < NR:
-                load_x(s + PREFETCH)
+            if s + PREFETCH + 3 < NR:
+                load_x(s + PREFETCH + 3)
             store_round(o)
 
         s = NR - 1
@@ -278,7 +292,8 @@ def tile_mom_t_kernel(tc, x1, x2, x3, W, b, gamma, beta, running_mean, running_v
         for fb in range(4):
             affine(nc.gpsimd, s, fb, 0, H)
         transposes_out(s - 1, ())
-        store_round(s - 1)
+        for jj in (0, 2):
+            store(TB - 1, jj, jj + 2, D, 2 * D)
         for fb in range(4):
             affine(nc.vector, s, fb, H, D)
         for half in range(2):

@@ -21,7 +21,7 @@ TB = 8
 NR = TB * E
 FLOPS = 2 * TOKENS * D * D * E
 
-X_BUFS = 20
+X_BUFS = 18
 PREFETCH = 16
 ON_VECTOR = (3,)
 
@@ -37,7 +37,7 @@ def tile_mom_t_kernel(tc, x1, x2, x3, W, b, gamma, beta, running_mean, running_v
         xin_pool = ctx.enter_context(tc.tile_pool(name="xin", bufs=X_BUFS))
         grp_pool = ctx.enter_context(tc.tile_pool(name="grp", bufs=3))
         q_pool = ctx.enter_context(tc.tile_pool(name="q", bufs=3))
-        z_pool = ctx.enter_context(tc.tile_pool(name="z", bufs=3))
+        z_pool = ctx.enter_context(tc.tile_pool(name="z", bufs=4))
         st_pool = ctx.enter_context(tc.tile_pool(name="st", bufs=3))
         psum = ctx.enter_context(tc.psum_pool(name="psum", bufs=8))
         ctx.enter_context(tc.manual_schedule())
@@ -273,16 +273,21 @@ def tile_mom_t_kernel(tc, x1, x2, x3, W, b, gamma, beta, running_mean, running_v
             if s + 1 == 2:
                 quantise_w(2)
             quantise_x(s + 1)
+            o = s - 2
+            if o >= 0:
+                transposes_out(o, (0, 1))
             if s + 2 < NR:
                 transposes_in(xin[s + 2], "x%d" % (s + 2), "VV")
-            o = s - 1
-            transposes_out(o, (0, 1))
+            if s == NR - 2:
+                transposes_out(s - 1, (0,))
             affine_on_vector(s)
             if s + PREFETCH + 3 < NR:
                 load_x(s + PREFETCH + 3)
-            store_round(o)
+            if o >= 0:
+                store_round(o)
 
         s = NR - 1
+        store_round(s - 2)
         products(s)
         zt[s] = z_pool.tile([P, 4, D], F32, name="z%d" % s, tag="z")
         H = D // 2

@@ -23,7 +23,8 @@ FLOPS = 2 * TOKENS * D * D * E
 
 X_BUFS = 18
 PREFETCH = 16
-ON_VECTOR = (3,)
+CATCH_UP = NR - 4
+ON_VECTOR = ((0,), (0, 1))
 
 
 def tile_mom_t_kernel(tc, x1, x2, x3, W, b, gamma, beta, running_mean, running_var, out):
@@ -45,12 +46,6 @@ def tile_mom_t_kernel(tc, x1, x2, x3, W, b, gamma, beta, running_mean, running_v
         warm = const.tile([P, 1], F32, name="warm")
         nc.vector.memset(warm[:], 0.0)
         nc.scalar.activation(out=warm[:], in_=warm[:], func=ACT.Gelu_apprx_sigmoid)
-
-        zeros = const.tile([P, D], BF16, name="zeros")
-        nc.gpsimd.memset(zeros[:], 0.0)
-        idle = psum.tile([P, D], F32, name="idle", tag="bank")
-        for i in range(2):
-            nc.tensor.matmul(idle[:], lhsT=zeros[:, 0:P], rhs=zeros[:], start=True, stop=True)
 
         ident = const.tile([P, P], F32, name="ident")
         make_identity(nc, ident[:])
@@ -151,15 +146,19 @@ def tile_mom_t_kernel(tc, x1, x2, x3, W, b, gamma, beta, running_mean, running_v
             par["s"] = const.tile([P, 12], F32, name="s_t")
             par["t"] = const.tile([P, 12], F32, name="t_t")
 
-        def params_affine(c0, c1):
+        def params_rsqrt():
+            rs = const.tile([P, 12], F32, name="rs")
+            nc.gpsimd.tensor_scalar_add(out=rs[:], in0=par["b"][:, 64:76], scalar1=EPS)
+            nc.gpsimd.tensor_tensor(out=rs[:], in0=rs[:], in1=mhalf[:], op=ALU.pow)
+            par["rs"] = rs
+
+        def params_affine():
             pt = par["b"]
-            s_t = par["s"][:, c0:c1]
-            t_t = par["t"][:, c0:c1]
-            nc.gpsimd.tensor_scalar_add(out=s_t, in0=pt[:, 64 + c0 : 64 + c1], scalar1=EPS)
-            nc.gpsimd.tensor_tensor(out=s_t, in0=s_t, in1=mhalf[:, c0:c1], op=ALU.pow)
-            nc.gpsimd.tensor_mul(out=s_t, in0=s_t, in1=pt[:, 16 + c0 : 16 + c1])
-            nc.gpsimd.tensor_mul(out=t_t, in0=pt[:, 48 + c0 : 48 + c1], in1=s_t)
-            nc.gpsimd.tensor_sub(out=t_t, in0=pt[:, 32 + c0 : 32 + c1], in1=t_t)
+            s_t = par["s"][:]
+            t_t = par["t"][:]
+            nc.vector.tensor_mul(out=s_t, in0=par["rs"][:], in1=pt[:, 16:28])
+            nc.vector.tensor_mul(out=t_t, in0=pt[:, 48:60], in1=s_t)
+            nc.vector.tensor_sub(out=t_t, in0=pt[:, 32:44], in1=t_t)
 
         accs = {}
 
@@ -194,16 +193,13 @@ def tile_mom_t_kernel(tc, x1, x2, x3, W, b, gamma, beta, running_mean, running_v
                 op0=ALU.mult, op1=ALU.add,
             )
 
-        def activate(s):
-            zt[s] = z_pool.tile([P, 4, D], F32, name="z%d" % s, tag="z")
+        def affine_on_gpsimd(s):
             for fb in range(4):
-                gelu(s, fb, 0, D)
-            for fb in range(4):
-                if fb not in ON_VECTOR:
+                if fb not in ON_VECTOR[s % 2]:
                     affine(nc.gpsimd, s, fb, 0, D)
 
         def affine_on_vector(s):
-            for fb in ON_VECTOR:
+            for fb in ON_VECTOR[s % 2]:
                 affine(nc.vector, s, fb, 0, D)
 
         def out_bank(o, jj):
@@ -238,7 +234,7 @@ def tile_mom_t_kernel(tc, x1, x2, x3, W, b, gamma, beta, running_mean, running_v
 
         def store_round(o):
             tb, e = divmod(o, E)
-            if tb >= TB - 2:
+            if tb >= TB - 4:
                 store(tb, 0, 4, e * D, (e + 1) * D)
             elif e == E - 1:
                 store(tb, 0, 4, 0, E * D)
@@ -253,8 +249,7 @@ def tile_mom_t_kernel(tc, x1, x2, x3, W, b, gamma, beta, running_mean, running_v
         quantise_w(1)
         params_transpose()
         params_columns()
-        params_affine(0, 4)
-        params_affine(4, 12)
+        params_rsqrt()
         products(0)
         zt[0] = z_pool.tile([P, 4, D], F32, name="z0", tag="z")
         for fb in range(4):
@@ -262,32 +257,34 @@ def tile_mom_t_kernel(tc, x1, x2, x3, W, b, gamma, beta, running_mean, running_v
         quantise_x(1)
         transposes_in(win[2], "w2", "SV")
         transposes_in(xin[2], "x2", "VV")
-        for fb in range(4):
-            affine(nc.vector, 0, fb, 0, D)
-        for r in range(PREFETCH, PREFETCH + 4):
-            load_x(r)
+        load_x(PREFETCH)
 
         for s in range(1, NR - 1):
             products(s)
-            activate(s)
-            if s + 1 == 2:
+            zt[s] = z_pool.tile([P, 4, D], F32, name="z%d" % s, tag="z")
+            for fb in range(4):
+                gelu(s, fb, 0, D)
+            if s == 1:
                 quantise_w(2)
             quantise_x(s + 1)
-            o = s - 2
-            if o >= 0:
-                transposes_out(o, (0, 1))
+            if s == 1:
+                params_affine()
+                for fb in range(4):
+                    affine(nc.vector, 0, fb, 0, D)
+            affine_on_gpsimd(s)
+            if 2 <= s <= CATCH_UP:
+                transposes_out(s - 2, (0, 1))
+                store_round(s - 2)
             if s + 2 < NR:
                 transposes_in(xin[s + 2], "x%d" % (s + 2), "VV")
-            if s == NR - 2:
-                transposes_out(s - 1, (0,))
+            if s >= CATCH_UP:
+                transposes_out(s - 1, (0, 1))
+                store_round(s - 1)
             affine_on_vector(s)
-            if s + PREFETCH + 3 < NR:
-                load_x(s + PREFETCH + 3)
-            if o >= 0:
-                store_round(o)
+            if s + PREFETCH < NR:
+                load_x(s + PREFETCH)
 
         s = NR - 1
-        store_round(s - 2)
         products(s)
         zt[s] = z_pool.tile([P, 4, D], F32, name="z%d" % s, tag="z")
         H = D // 2

@@ -24,7 +24,7 @@ FLOPS = 2 * TOKENS * D * D * E
 X_BUFS = 18
 PREFETCH = 16
 CATCH_UP = NR - 4
-ON_VECTOR = ((0,), (0, 1))
+SPLIT = 256
 
 
 def tile_mom_t_kernel(tc, x1, x2, x3, W, b, gamma, beta, running_mean, running_var, out):
@@ -194,13 +194,13 @@ def tile_mom_t_kernel(tc, x1, x2, x3, W, b, gamma, beta, running_mean, running_v
             )
 
         def affine_on_gpsimd(s):
-            for fb in range(4):
-                if fb not in ON_VECTOR[s % 2]:
-                    affine(nc.gpsimd, s, fb, 0, D)
+            affine(nc.gpsimd, s, 1, SPLIT, D)
+            affine(nc.gpsimd, s, 2, 0, D)
+            affine(nc.gpsimd, s, 3, 0, D)
 
         def affine_on_vector(s):
-            for fb in ON_VECTOR[s % 2]:
-                affine(nc.vector, s, fb, 0, D)
+            affine(nc.vector, s, 0, 0, D)
+            affine(nc.vector, s, 1, 0, SPLIT)
 
         def out_bank(o, jj):
             bank = psum.tile([P, D], F32, name="o%d_%d" % (o, jj), tag="bank")

from contextlib import ExitStack

import concourse.mybir as mybir
from concourse.masks import make_identity

F32 = mybir.dt.float32
BF16 = mybir.dt.bfloat16
U32 = mybir.dt.uint32
U8 = mybir.dt.uint8
FP8X4 = mybir.dt.float8_e4m3fn_x4
ACT = mybir.ActivationFunctionType
ALU = mybir.AluOpType

P = 128
TOKENS = 4096
D = 512
E = 3
EPS = 1e-5
JT = TOKENS // P
TB = 8
NR = TB * E
FLOPS = 2 * TOKENS * D * D * E

X_BUFS = 18
PREFETCH = 16
CATCH_UP = NR - 4
SPLIT = 256


def tile_mom_t_kernel(tc, x1, x2, x3, W, b, gamma, beta, running_mean, running_var, out):
    nc = tc.nc
    xs = [x.rearrange("(p j) k -> p (j k)", j=JT) for x in (x1, x2, x3)]
    w_rows = W.rearrange("o e f k -> (o e f) k")
    out_v = out.rearrange("(p j) c -> p j c", j=JT)

    with ExitStack() as ctx:
        const = ctx.enter_context(tc.tile_pool(name="const", bufs=1))
        xin_pool = ctx.enter_context(tc.tile_pool(name="xin", bufs=X_BUFS))
        grp_pool = ctx.enter_context(tc.tile_pool(name="grp", bufs=3))
        q_pool = ctx.enter_context(tc.tile_pool(name="q", bufs=3))
        z_pool = ctx.enter_context(tc.tile_pool(name="z", bufs=4))
        st_pool = ctx.enter_context(tc.tile_pool(name="st", bufs=3))
        psum = ctx.enter_context(tc.psum_pool(name="psum", bufs=8))
        ctx.enter_context(tc.manual_schedule())

        warm = const.tile([P, 1], F32, name="warm")
        nc.vector.memset(warm[:], 0.0)
        nc.scalar.activation(out=warm[:], in_=warm[:], func=ACT.Gelu_apprx_sigmoid)

        ident = const.tile([P, P], F32, name="ident")
        make_identity(nc, ident[:])
        mhalf = const.tile([P, 12], F32, name="mhalf")
        nc.gpsimd.memset(mhalf[:], -0.5)

        prow = const.tile([P, P], BF16, name="prow")
        nc.vector.memset(prow[:], 0.0)
        for i, v in enumerate((b, gamma, beta, running_mean, running_var)):
            nc.scalar.dma_start(out=prow[16 * i : 16 * i + 12, :], in_=v.rearrange("o e (q c) -> (o e q) c", c=P))

        xin = {}
        win = {}

        def load_w(e):
            t = xin_pool.tile([P, 4 * D], BF16, name="win%d" % e, tag="xin")
            cuts = (0, 1, 2, 4) if e == 0 else (0, 4)
            for lo, hi in zip(cuts[:-1], cuts[1:]):
                nc.sync.dma_start(
                    out=t[:].rearrange("p (q k) -> p q k", q=4)[:, lo:hi, :],
                    in_=w_rows[e * D + lo * P : e * D + hi * P, :].rearrange("(q p) k -> p q k", p=P),
                )
            win[e] = t

        def load_x(r):
            tb, e = divmod(r, E)
            t = xin_pool.tile([P, 4 * D], BF16, name="xin%d" % r, tag="xin")
            cuts = (0, 2, 4) if r == 0 else (0, 4)
            for lo, hi in zip(cuts[:-1], cuts[1:]):
                nc.sync.dma_start(out=t[:, lo * D : hi * D], in_=xs[e][:, (tb * 4 + lo) * D : (tb * 4 + hi) * D])
            xin[r] = t

        for e in range(E):
            load_w(e)
            load_x(e)
        for r in range(E, PREFETCH):
            load_x(r)

        w_codes = [const.tile([P, D], U32, name="wc%d" % e, align_bytes=64) for e in range(E)]
        w_scales = [const.tile([P, D], U8, name="ws%d" % e, align_bytes=64) for e in range(E)]
        grouped = {}
        codes = {}
        scales = {}
        zt = {}
        stage = {}
        par = {}

        def transposes_in(src, key, engines):
            sf = src[:].bitcast(F32)
            g = grp_pool.tile([P, 4 * D], BF16, name="g_%s" % key, tag="g", align_bytes=64)
            gf = g[:].bitcast(F32)
            banks = []
            for h in range(2):
                bank = psum.tile([P, D], F32, name="a_%s_%d" % (key, h), tag="bank")
                for jj in (2 * h, 2 * h + 1):
                    for u in range(2):
                        nc.tensor.transpose(
                            bank[:, u * 256 + (jj % 2) * P : u * 256 + (jj % 2) * P + P],
                            sf[:, jj * 256 + u : (jj + 1) * 256 : 2],
                            ident[:],
                        )
                banks.append(bank)
            for h in range(2):
                copy_bank(engines[h], gf[:, h * D : (h + 1) * D].rearrange("p (c u) -> p c u", u=2),
                          banks[h][:].rearrange("p (u c) -> p c u", u=2))
            grouped[key] = g

        def copy_bank(engine, dst, src):
            if engine == "S":
                nc.scalar.copy(out=dst, in_=src)
            else:
                nc.vector.tensor_copy(out=dst, in_=src)

        def quantise_w(e):
            nc.vector.quantize_mx(out=w_codes[e][:].bitcast(FP8X4), scales=w_scales[e][:], in_=grouped["w%d" % e][:])

        def quantise_x(q):
            c_t = q_pool.tile([P, D], U32, name="c%d" % q, tag="c", align_bytes=64)
            s_t2 = q_pool.tile([P, D], U8, name="s%d" % q, tag="s", align_bytes=64)
            nc.vector.quantize_mx(out=c_t[:].bitcast(FP8X4), scales=s_t2[:], in_=grouped["x%d" % q][:])
            codes[q] = c_t
            scales[q] = s_t2

        def params_transpose():
            bank = psum.tile([P, D], F32, name="pbank", tag="bank")
            nc.tensor.transpose(bank[:, 0:P], par["pf"][:], ident[:])
            par["bank"] = bank

        def params_cast():
            pf = const.tile([P, P], F32, name="pf")
            nc.gpsimd.tensor_copy(out=pf[:], in_=prow[:])
            par["pf"] = pf

        def params_columns():
            pt = const.tile([P, P], F32, name="pt")
            nc.scalar.copy(out=pt[:], in_=par["bank"][:, 0:P])
            par["b"] = pt
            par["s"] = const.tile([P, 12], F32, name="s_t")
            par["t"] = const.tile([P, 12], F32, name="t_t")

        def params_rsqrt():
            rs = const.tile([P, 12], F32, name="rs")
            nc.gpsimd.tensor_scalar_add(out=rs[:], in0=par["b"][:, 64:76], scalar1=EPS)
            nc.gpsimd.tensor_tensor(out=rs[:], in0=rs[:], in1=mhalf[:], op=ALU.pow)
            par["rs"] = rs

        def params_affine():
            pt = par["b"]
            s_t = par["s"][:]
            t_t = par["t"][:]
            nc.vector.tensor_mul(out=s_t, in0=par["rs"][:], in1=pt[:, 16:28])
            nc.vector.tensor_mul(out=t_t, in0=pt[:, 48:60], in1=s_t)
            nc.vector.tensor_sub(out=t_t, in0=pt[:, 32:44], in1=t_t)

        accs = {}

        def products(s):
            e = s % E
            accs[s] = []
            for fb in range(4):
                acc = psum.tile([P, D], F32, name="acc%d_%d" % (s, fb), tag="bank")
                nc.tensor.matmul_mx(
                    out=acc[:],
                    lhsT=w_codes[e][:, fb * P : (fb + 1) * P].bitcast(FP8X4),
                    lhsT_scale=w_scales[e][:, fb * P : (fb + 1) * P],
                    rhs=codes[s][:].bitcast(FP8X4),
                    rhs_scale=scales[s][:],
                    start=True,
                    stop=True,
                )
                accs[s].append(acc)

        def gelu(s, fb, t0, t1):
            col = s % E * 4 + fb
            nc.scalar.activation(
                out=zt[s][:, fb, t0:t1], in_=accs[s][fb][:, t0:t1], func=ACT.Gelu_apprx_sigmoid,
                bias=par["b"][:, col : col + 1], scale=1.0,
            )

        def affine(engine, s, fb, t0, t1):
            col = s % E * 4 + fb
            engine.tensor_scalar(
                out=zt[s][:, fb, t0:t1], in0=zt[s][:, fb, t0:t1],
                scalar1=par["s"][:, col : col + 1], scalar2=par["t"][:, col : col + 1],
                op0=ALU.mult, op1=ALU.add,
            )

        def affine_on_gpsimd(s):
            affine(nc.gpsimd, s, 1, SPLIT, D)
            affine(nc.gpsimd, s, 2, 0, D)
            affine(nc.gpsimd, s, 3, 0, D)

        def affine_on_vector(s):
            affine(nc.vector, s, 0, 0, D)
            affine(nc.vector, s, 1, 0, SPLIT)

        def out_bank(o, jj):
            bank = psum.tile([P, D], F32, name="o%d_%d" % (o, jj), tag="bank")
            return bank

        def back_transpose(o, bank, jj, fb):
            nc.tensor.transpose(bank[:, fb * P : (fb + 1) * P], zt[o][:, fb, jj * P : (jj + 1) * P], ident[:])

        def out_copy(o, bank, jj, engine):
            tb, e = divmod(o, E)
            copy_bank(engine, stage[tb][:, jj * E * D + e * D : jj * E * D + (e + 1) * D], bank[:])

        def transposes_out(o, on_scalar):
            tb, e = divmod(o, E)
            if e == 0:
                stage[tb] = st_pool.tile([P, 4 * E * D], F32, name="st%d" % tb, tag="st")
            banks = []
            for jj in range(4):
                bank = out_bank(o, jj)
                for fb in range(4):
                    back_transpose(o, bank, jj, fb)
                banks.append(bank)
            for jj in range(4):
                out_copy(o, banks[jj], jj, "S" if jj in on_scalar else "V")

        def store(tb, lo, hi, c0, c1):
            nc.sync.dma_start(
                out=out_v[:, tb * 4 + lo : tb * 4 + hi, c0:c1],
                in_=stage[tb][:].rearrange("p (j c) -> p j c", j=4)[:, lo:hi, c0:c1],
            )

        def store_round(o):
            tb, e = divmod(o, E)
            if tb >= TB - 4:
                store(tb, 0, 4, e * D, (e + 1) * D)
            elif e == E - 1:
                store(tb, 0, 4, 0, E * D)

        params_cast()
        transposes_in(win[0], "w0", "VS")
        transposes_in(xin[0], "x0", "VS")
        quantise_w(0)
        quantise_x(0)
        transposes_in(win[1], "w1", "SS")
        transposes_in(xin[1], "x1", "VV")
        quantise_w(1)
        params_transpose()
        params_columns()
        params_rsqrt()
        products(0)
        zt[0] = z_pool.tile([P, 4, D], F32, name="z0", tag="z")
        for fb in range(4):
            gelu(0, fb, 0, D)
        quantise_x(1)
        transposes_in(win[2], "w2", "SV")
        transposes_in(xin[2], "x2", "VV")
        load_x(PREFETCH)

        for s in range(1, NR - 1):
            products(s)
            zt[s] = z_pool.tile([P, 4, D], F32, name="z%d" % s, tag="z")
            for fb in range(4):
                gelu(s, fb, 0, D)
            if s == 1:
                quantise_w(2)
            quantise_x(s + 1)
            if s == 1:
                params_affine()
                for fb in range(4):
                    affine(nc.vector, 0, fb, 0, D)
            affine_on_gpsimd(s)
            if 2 <= s <= CATCH_UP:
                transposes_out(s - 2, (0, 1))
                store_round(s - 2)
            if s + 2 < NR:
                transposes_in(xin[s + 2], "x%d" % (s + 2), "VV")
            if s >= CATCH_UP:
                transposes_out(s - 1, (0, 1))
                store_round(s - 1)
            affine_on_vector(s)
            if s + PREFETCH < NR:
                load_x(s + PREFETCH)

        s = NR - 1
        products(s)
        zt[s] = z_pool.tile([P, 4, D], F32, name="z%d" % s, tag="z")
        H = D // 2
        for half in range(2):
            for fb in range(4):
                gelu(s, fb, half * H, half * H + H)
        for fb in range(4):
            affine(nc.gpsimd, s, fb, 0, H)
        transposes_out(s - 1, ())
        for jj in (0, 2):
            store(TB - 1, jj, jj + 2, D, 2 * D)
        for fb in range(4):
            affine(nc.vector, s, fb, H, D)
        for half in range(2):
            banks = [out_bank(s, 2 * half + i) for i in range(2)]
            for fb in range(4):
                for i in range(2):
                    back_transpose(s, banks[i], 2 * half + i, fb)
            for i in range(2):
                jj = 2 * half + i
                out_copy(s, banks[i], jj, "VS"[i])
                store(TB - 1, jj, jj + 1, 2 * D, 3 * D)
